import numpy as np
import ml_dtypes

BF16 = ml_dtypes.bfloat16


def bf(x):
    return np.asarray(x, np.float32).astype(BF16)


def f32(x):
    return np.asarray(x, np.float32)


def f64(x):
    return np.asarray(x).astype(np.float64)


def striped(idx):
    return np.tile(idx.reshape(-1, 16).T, (8, 1))


C, S, N = 512, 256, 128
P = 0.125


def setup_inputs():
    base = f32(np.random.standard_normal((C, S)))
    node = f32(np.random.standard_normal((C, N)))
    adj = np.maximum((np.random.random((N, N)) < P).astype(np.float32), np.eye(N, dtype=np.float32))
    wc = bf(np.random.standard_normal((C, C)) / np.sqrt(C))
    return {"base": base, "node": node, "adj": bf(adj), "wc": wc, "offs": striped(np.random.permutation(S)[:N])}


def reference(base, node, adj, wc, offs):
    idx = offs[:16].T.reshape(-1)
    x = f64(node)
    a = f64(adj)
    deg = a.sum(axis=0, keepdims=True)
    h = x.T @ f64(wc)
    ctx = (h.T @ a) / deg
    res = f64(base).copy()
    res[:, idx] = x + ctx
    return res

@@ -1,0 +1,53 @@
+import concourse.mybir as mybir
+
+F32, BF16, U16 = mybir.dt.float32, mybir.dt.bfloat16, mybir.dt.uint16
+ADD, MULT = mybir.AluOpType.add, mybir.AluOpType.mult
+
+P = 128
+C, S, N = 512, 256, 128
+CB = C // P
+
+FLOPS = 2 * N * C * C + 2 * C * N * N
+
+
+def tile_attngcnlayer_kernel(tc, base, node, adj, wc, offs, out):
+    nc = tc.nc
+    with (
+        tc.tile_pool(name="held", bufs=1) as held,
+        tc.psum_pool(name="psum", bufs=1) as psum,
+    ):
+        offsets = held.tile([P, N // 16], U16, name="offsets")
+        nc.sync.dma_start(offsets[:], offs)
+        node_f32 = held.tile([P, CB, N], F32, name="node_f32")
+        nc.sync.dma_start(node_f32[:], node.rearrange("(b p) j -> p b j", p=P))
+        wc_bf = held.tile([P, CB, C], BF16, name="wc_bf")
+        nc.scalar.dma_start(wc_bf[:], wc.rearrange("(b p) c -> p b c", p=P))
+        adj_bf = held.tile([P, N], BF16, name="adj_bf")
+        nc.sync.dma_start(adj_bf[:], adj)
+        windows = [held.tile([P, S], F32, name=f"window{b}") for b in range(CB)]
+        for b in range(CB):
+            nc.gpsimd.dma_start(windows[b][:], base[b * P : (b + 1) * P, :])
+
+        ones = held.tile([P, P], BF16, name="ones")
+        nc.gpsimd.memset(ones[:], 1.0)
+        deg_ps = psum.tile([P, N], F32, name="deg_ps")
+        nc.tensor.matmul(deg_ps[:], ones[:], adj_bf[:], start=True, stop=True)
+        inv_deg = held.tile([P, N], F32, name="inv_deg")
+        nc.vector.reciprocal(inv_deg[:], deg_ps[:])
+
+        node_bf = held.tile([P, CB, N], BF16, name="node_bf")
+        nc.vector.tensor_copy(node_bf[:], node_f32[:])
+        h_ps = psum.tile([P, C], F32, name="h_ps")
+        for k in range(CB):
+            nc.tensor.matmul(h_ps[:], node_bf[:, k, :], wc_bf[:, k, :], start=(k == 0), stop=(k == CB - 1))
+        h_bf = held.tile([P, C], BF16, name="h_bf")
+        nc.vector.tensor_copy(h_bf[:], h_ps[:])
+
+        for b in range(CB):
+            ctx_ps = psum.tile([P, N], F32, name=f"ctx_ps{b}")
+            nc.tensor.matmul(ctx_ps[:], h_bf[:, b * P : (b + 1) * P], adj_bf[:], start=True, stop=True)
+            ctx = held.tile([P, N], F32, name=f"ctx{b}")
+            nc.vector.tensor_tensor(ctx[:], ctx_ps[:], inv_deg[:], MULT)
+            nc.vector.tensor_tensor(windows[b][:].indirect(offsets[:]), node_f32[:, b, :], ctx[:], ADD)
+            store_queue = nc.sync if b % 2 == 0 else nc.scalar
+            store_queue.dma_start(out[b * P : (b + 1) * P, :], windows[b][:])

@@ -18,15 +18,17 @@ def tile_attngcnlayer_kernel(tc, base, node, adj, wc, offs, out):
     ):
         offsets = held.tile([P, N // 16], U16, name="offsets")
         nc.sync.dma_start(offsets[:], offs)
-        node_f32 = held.tile([P, CB, N], F32, name="node_f32")
-        nc.sync.dma_start(node_f32[:], node.rearrange("(b p) j -> p b j", p=P))
-        wc_bf = held.tile([P, CB, C], BF16, name="wc_bf")
-        nc.scalar.dma_start(wc_bf[:], wc.rearrange("(b p) c -> p b c", p=P))
         adj_bf = held.tile([P, N], BF16, name="adj_bf")
         nc.sync.dma_start(adj_bf[:], adj)
+        node_f32 = held.tile([P, CB, N], F32, name="node_f32")
+        wc_bf = held.tile([P, CB, C], BF16, name="wc_bf")
+        for k in range(CB):
+            nc.sync.dma_start(node_f32[:, k, :], node[k * P : (k + 1) * P, :])
+            nc.scalar.dma_start(wc_bf[:, k, :], wc[k * P : (k + 1) * P, :])
         windows = [held.tile([P, S], F32, name=f"window{b}") for b in range(CB)]
         for b in range(CB):
-            nc.gpsimd.dma_start(windows[b][:], base[b * P : (b + 1) * P, :])
+            load_queue = nc.sync if b % 2 == 0 else nc.scalar
+            load_queue.dma_start(windows[b][:], base[b * P : (b + 1) * P, :])
 
         ones = held.tile([P, P], BF16, name="ones")
         nc.gpsimd.memset(ones[:], 1.0)
@@ -36,9 +38,9 @@ def tile_attngcnlayer_kernel(tc, base, node, adj, wc, offs, out):
         nc.vector.reciprocal(inv_deg[:], deg_ps[:])
 
         node_bf = held.tile([P, CB, N], BF16, name="node_bf")
-        nc.vector.tensor_copy(node_bf[:], node_f32[:])
         h_ps = psum.tile([P, C], F32, name="h_ps")
         for k in range(CB):
+            nc.vector.tensor_copy(node_bf[:, k, :], node_f32[:, k, :])
             nc.tensor.matmul(h_ps[:], node_bf[:, k, :], wc_bf[:, k, :], start=(k == 0), stop=(k == CB - 1))
         h_bf = held.tile([P, C], BF16, name="h_bf")
         nc.vector.tensor_copy(h_bf[:], h_ps[:])

@@ -2,6 +2,7 @@ import concourse.mybir as mybir
 
 F32, BF16, U16 = mybir.dt.float32, mybir.dt.bfloat16, mybir.dt.uint16
 ADD, MULT = mybir.AluOpType.add, mybir.AluOpType.mult
+COPY = mybir.ActivationFunctionType.Copy
 
 P = 128
 C, S, N = 512, 256, 128
@@ -14,42 +15,45 @@ def tile_attngcnlayer_kernel(tc, base, node, adj, wc, offs, out):
     nc = tc.nc
     with (
         tc.tile_pool(name="held", bufs=1) as held,
-        tc.psum_pool(name="psum", bufs=1) as psum,
+        tc.psum_pool(name="psum_deg", bufs=1) as psum_deg,
+        tc.psum_pool(name="psum", bufs=2) as psum,
     ):
         offsets = held.tile([P, N // 16], U16, name="offsets")
         nc.sync.dma_start(offsets[:], offs)
         adj_bf = held.tile([P, N], BF16, name="adj_bf")
         nc.sync.dma_start(adj_bf[:], adj)
         node_f32 = held.tile([P, CB, N], F32, name="node_f32")
-        wc_bf = held.tile([P, CB, C], BF16, name="wc_bf")
         for k in range(CB):
             nc.sync.dma_start(node_f32[:, k, :], node[k * P : (k + 1) * P, :])
-            nc.scalar.dma_start(wc_bf[:, k, :], wc[k * P : (k + 1) * P, :])
+        wc_by_rows = wc.rearrange("(k p) c -> p k c", p=P)
+        wc_bf = [held.tile([P, CB, P], BF16, name=f"wc_bf{b}") for b in range(CB)]
+        for b in range(CB):
+            nc.scalar.dma_start(wc_bf[b][:], wc_by_rows[:, :, b * P : (b + 1) * P])
         windows = [held.tile([P, S], F32, name=f"window{b}") for b in range(CB)]
         for b in range(CB):
-            load_queue = nc.sync if b % 2 == 0 else nc.scalar
-            load_queue.dma_start(windows[b][:], base[b * P : (b + 1) * P, :])
+            nc.sync.dma_start(windows[b][:], base[b * P : (b + 1) * P, :])
 
         ones = held.tile([P, P], BF16, name="ones")
         nc.gpsimd.memset(ones[:], 1.0)
-        deg_ps = psum.tile([P, N], F32, name="deg_ps")
+        deg_ps = psum_deg.tile([P, N], F32, name="deg_ps")
         nc.tensor.matmul(deg_ps[:], ones[:], adj_bf[:], start=True, stop=True)
         inv_deg = held.tile([P, N], F32, name="inv_deg")
         nc.vector.reciprocal(inv_deg[:], deg_ps[:])
 
         node_bf = held.tile([P, CB, N], BF16, name="node_bf")
-        h_ps = psum.tile([P, C], F32, name="h_ps")
         for k in range(CB):
             nc.vector.tensor_copy(node_bf[:, k, :], node_f32[:, k, :])
-            nc.tensor.matmul(h_ps[:], node_bf[:, k, :], wc_bf[:, k, :], start=(k == 0), stop=(k == CB - 1))
-        h_bf = held.tile([P, C], BF16, name="h_bf")
-        nc.vector.tensor_copy(h_bf[:], h_ps[:])
 
         for b in range(CB):
-            ctx_ps = psum.tile([P, N], F32, name=f"ctx_ps{b}")
-            nc.tensor.matmul(ctx_ps[:], h_bf[:, b * P : (b + 1) * P], adj_bf[:], start=True, stop=True)
+            h_ps = psum.tile([P, P], F32, name="h_ps")
+            for k in range(CB):
+                nc.tensor.matmul(h_ps[:], node_bf[:, k, :], wc_bf[b][:, k, :], start=(k == 0), stop=(k == CB - 1))
+            h_bf = held.tile([P, P], BF16, name=f"h_bf{b}")
+            nc.scalar.activation(h_bf[:], h_ps[:], COPY)
+
+            ctx_ps = psum.tile([P, N], F32, name="ctx_ps")
+            nc.tensor.matmul(ctx_ps[:], h_bf[:], adj_bf[:], start=True, stop=True)
             ctx = held.tile([P, N], F32, name=f"ctx{b}")
             nc.vector.tensor_tensor(ctx[:], ctx_ps[:], inv_deg[:], MULT)
             nc.vector.tensor_tensor(windows[b][:].indirect(offsets[:]), node_f32[:, b, :], ctx[:], ADD)
-            store_queue = nc.sync if b % 2 == 0 else nc.scalar
-            store_queue.dma_start(out[b * P : (b + 1) * P, :], windows[b][:])
+            nc.sync.dma_start(out[b * P : (b + 1) * P, :], windows[b][:])

@@ -37,12 +37,12 @@ def tile_attngcnlayer_kernel(tc, base, node, adj, wc, offs, out):
         nc.gpsimd.memset(ones[:], 1.0)
         deg_ps = psum_deg.tile([P, N], F32, name="deg_ps")
         nc.tensor.matmul(deg_ps[:], ones[:], adj_bf[:], start=True, stop=True)
-        inv_deg = held.tile([P, N], F32, name="inv_deg")
-        nc.vector.reciprocal(inv_deg[:], deg_ps[:])
 
         node_bf = held.tile([P, CB, N], BF16, name="node_bf")
         for k in range(CB):
             nc.vector.tensor_copy(node_bf[:, k, :], node_f32[:, k, :])
+        inv_deg = held.tile([P, N], F32, name="inv_deg")
+        nc.vector.reciprocal(inv_deg[:], deg_ps[:])
 
         for b in range(CB):
             h_ps = psum.tile([P, P], F32, name="h_ps")

@@ -7,6 +7,7 @@ COPY = mybir.ActivationFunctionType.Copy
 P = 128
 C, S, N = 512, 256, 128
 CB = C // P
+HALF = CB // 2
 
 FLOPS = 2 * N * C * C + 2 * C * N * N
 
@@ -18,31 +19,34 @@ def tile_attngcnlayer_kernel(tc, base, node, adj, wc, offs, out):
         tc.psum_pool(name="psum_deg", bufs=1) as psum_deg,
         tc.psum_pool(name="psum", bufs=2) as psum,
     ):
-        offsets = held.tile([P, N // 16], U16, name="offsets")
-        nc.sync.dma_start(offsets[:], offs)
-        adj_bf = held.tile([P, N], BF16, name="adj_bf")
-        nc.sync.dma_start(adj_bf[:], adj)
+        node_by_rows = node.rearrange("(k p) j -> p k j", p=P)
         node_f32 = held.tile([P, CB, N], F32, name="node_f32")
-        for k in range(CB):
-            nc.sync.dma_start(node_f32[:, k, :], node[k * P : (k + 1) * P, :])
+        nc.sync.dma_start(node_f32[:, 0:HALF, :], node_by_rows[:, 0:HALF, :])
+        nc.scalar.dma_start(node_f32[:, HALF:CB, :], node_by_rows[:, HALF:CB, :])
         wc_by_rows = wc.rearrange("(k p) c -> p k c", p=P)
         wc_bf = [held.tile([P, CB, P], BF16, name=f"wc_bf{b}") for b in range(CB)]
-        for b in range(CB):
-            nc.scalar.dma_start(wc_bf[b][:], wc_by_rows[:, :, b * P : (b + 1) * P])
+        nc.sync.dma_start(wc_bf[0][:], wc_by_rows[:, :, 0:P])
+        adj_bf = held.tile([P, N], BF16, name="adj_bf")
+        nc.scalar.dma_start(adj_bf[:], adj)
+        offsets = held.tile([P, N // 16], U16, name="offsets")
+        nc.sync.dma_start(offsets[:], offs)
+        for b in range(1, CB):
+            nc.sync.dma_start(wc_bf[b][:], wc_by_rows[:, :, b * P : (b + 1) * P])
         windows = [held.tile([P, S], F32, name=f"window{b}") for b in range(CB)]
         for b in range(CB):
-            nc.sync.dma_start(windows[b][:], base[b * P : (b + 1) * P, :])
+            base_queue = nc.scalar if b < HALF else nc.gpsimd
+            base_queue.dma_start(windows[b][:], base[b * P : (b + 1) * P, :])
 
         ones = held.tile([P, P], BF16, name="ones")
         nc.gpsimd.memset(ones[:], 1.0)
         deg_ps = psum_deg.tile([P, N], F32, name="deg_ps")
         nc.tensor.matmul(deg_ps[:], ones[:], adj_bf[:], start=True, stop=True)
-
-        node_bf = held.tile([P, CB, N], BF16, name="node_bf")
-        for k in range(CB):
-            nc.vector.tensor_copy(node_bf[:, k, :], node_f32[:, k, :])
         inv_deg = held.tile([P, N], F32, name="inv_deg")
         nc.vector.reciprocal(inv_deg[:], deg_ps[:])
+
+        node_bf = held.tile([P, CB, N], BF16, name="node_bf")
+        nc.vector.tensor_copy(node_bf[:, 0:HALF, :], node_f32[:, 0:HALF, :])
+        nc.vector.tensor_copy(node_bf[:, HALF:CB, :], node_f32[:, HALF:CB, :])
 
         for b in range(CB):
             h_ps = psum.tile([P, P], F32, name="h_ps")

@@ -24,17 +24,16 @@ def tile_attngcnlayer_kernel(tc, base, node, adj, wc, offs, out):
         nc.sync.dma_start(node_f32[:, 0:HALF, :], node_by_rows[:, 0:HALF, :])
         nc.scalar.dma_start(node_f32[:, HALF:CB, :], node_by_rows[:, HALF:CB, :])
         wc_by_rows = wc.rearrange("(k p) c -> p k c", p=P)
-        wc_bf = [held.tile([P, CB, P], BF16, name=f"wc_bf{b}") for b in range(CB)]
-        nc.sync.dma_start(wc_bf[0][:], wc_by_rows[:, :, 0:P])
+        wc_bf = [held.tile([P, CB, HALF * P], BF16, name=f"wc_bf{half}") for half in range(2)]
+        nc.sync.dma_start(wc_bf[0][:], wc_by_rows[:, :, 0 : HALF * P])
         adj_bf = held.tile([P, N], BF16, name="adj_bf")
         nc.scalar.dma_start(adj_bf[:], adj)
         offsets = held.tile([P, N // 16], U16, name="offsets")
         nc.sync.dma_start(offsets[:], offs)
-        for b in range(1, CB):
-            nc.sync.dma_start(wc_bf[b][:], wc_by_rows[:, :, b * P : (b + 1) * P])
+        nc.sync.dma_start(wc_bf[1][:], wc_by_rows[:, :, HALF * P : C])
         windows = [held.tile([P, S], F32, name=f"window{b}") for b in range(CB)]
         for b in range(CB):
-            base_queue = nc.scalar if b < HALF else nc.gpsimd
+            base_queue = nc.scalar if b < HALF else nc.sync
             base_queue.dma_start(windows[b][:], base[b * P : (b + 1) * P, :])
 
         ones = held.tile([P, P], BF16, name="ones")
@@ -50,8 +49,9 @@ def tile_attngcnlayer_kernel(tc, base, node, adj, wc, offs, out):
 
         for b in range(CB):
             h_ps = psum.tile([P, P], F32, name="h_ps")
+            wc_cols = wc_bf[b // HALF][:, :, (b % HALF) * P : (b % HALF + 1) * P]
             for k in range(CB):
-                nc.tensor.matmul(h_ps[:], node_bf[:, k, :], wc_bf[b][:, k, :], start=(k == 0), stop=(k == CB - 1))
+                nc.tensor.matmul(h_ps[:], node_bf[:, k, :], wc_cols[:, k, :], start=(k == 0), stop=(k == CB - 1))
             h_bf = held.tile([P, P], BF16, name=f"h_bf{b}")
             nc.scalar.activation(h_bf[:], h_ps[:], COPY)
 

@@ -30,11 +30,11 @@ def tile_attngcnlayer_kernel(tc, base, node, adj, wc, offs, out):
         nc.scalar.dma_start(adj_bf[:], adj)
         offsets = held.tile([P, N // 16], U16, name="offsets")
         nc.sync.dma_start(offsets[:], offs)
-        nc.sync.dma_start(wc_bf[1][:], wc_by_rows[:, :, HALF * P : C])
         windows = [held.tile([P, S], F32, name=f"window{b}") for b in range(CB)]
-        for b in range(CB):
-            base_queue = nc.scalar if b < HALF else nc.sync
-            base_queue.dma_start(windows[b][:], base[b * P : (b + 1) * P, :])
+        nc.sync.dma_start(windows[0][:], base[0:P, :])
+        nc.sync.dma_start(wc_bf[1][:], wc_by_rows[:, :, HALF * P : C])
+        for b in range(1, CB):
+            nc.sync.dma_start(windows[b][:], base[b * P : (b + 1) * P, :])
 
         ones = held.tile([P, P], BF16, name="ones")
         nc.gpsimd.memset(ones[:], 1.0)

@@ -25,7 +25,8 @@ def tile_attngcnlayer_kernel(tc, base, node, adj, wc, offs, out):
         nc.scalar.dma_start(node_f32[:, HALF:CB, :], node_by_rows[:, HALF:CB, :])
         wc_by_rows = wc.rearrange("(k p) c -> p k c", p=P)
         wc_bf = [held.tile([P, CB, HALF * P], BF16, name=f"wc_bf{half}") for half in range(2)]
-        nc.sync.dma_start(wc_bf[0][:], wc_by_rows[:, :, 0 : HALF * P])
+        nc.sync.dma_start(wc_bf[0][:, 0:HALF, :], wc_by_rows[:, 0:HALF, 0 : HALF * P])
+        nc.sync.dma_start(wc_bf[0][:, HALF:CB, :], wc_by_rows[:, HALF:CB, 0 : HALF * P])
         adj_bf = held.tile([P, N], BF16, name="adj_bf")
         nc.scalar.dma_start(adj_bf[:], adj)
         offsets = held.tile([P, N // 16], U16, name="offsets")

@@ -23,12 +23,12 @@ def tile_attngcnlayer_kernel(tc, base, node, adj, wc, offs, out):
         node_f32 = held.tile([P, CB, N], F32, name="node_f32")
         nc.sync.dma_start(node_f32[:, 0:HALF, :], node_by_rows[:, 0:HALF, :])
         nc.scalar.dma_start(node_f32[:, HALF:CB, :], node_by_rows[:, HALF:CB, :])
+        adj_bf = held.tile([P, N], BF16, name="adj_bf")
+        nc.sync.dma_start(adj_bf[:], adj)
         wc_by_rows = wc.rearrange("(k p) c -> p k c", p=P)
         wc_bf = [held.tile([P, CB, HALF * P], BF16, name=f"wc_bf{half}") for half in range(2)]
         nc.sync.dma_start(wc_bf[0][:, 0:HALF, :], wc_by_rows[:, 0:HALF, 0 : HALF * P])
         nc.sync.dma_start(wc_bf[0][:, HALF:CB, :], wc_by_rows[:, HALF:CB, 0 : HALF * P])
-        adj_bf = held.tile([P, N], BF16, name="adj_bf")
-        nc.scalar.dma_start(adj_bf[:], adj)
         offsets = held.tile([P, N // 16], U16, name="offsets")
         nc.sync.dma_start(offsets[:], offs)
         windows = [held.tile([P, S], F32, name=f"window{b}") for b in range(CB)]

@@ -21,13 +21,13 @@ def tile_attngcnlayer_kernel(tc, base, node, adj, wc, offs, out):
     ):
         node_by_rows = node.rearrange("(k p) j -> p k j", p=P)
         node_f32 = held.tile([P, CB, N], F32, name="node_f32")
-        nc.sync.dma_start(node_f32[:, 0:HALF, :], node_by_rows[:, 0:HALF, :])
-        nc.scalar.dma_start(node_f32[:, HALF:CB, :], node_by_rows[:, HALF:CB, :])
+        nc.sync.dma_start(node_f32[:], node_by_rows)
         adj_bf = held.tile([P, N], BF16, name="adj_bf")
         nc.sync.dma_start(adj_bf[:], adj)
         wc_by_rows = wc.rearrange("(k p) c -> p k c", p=P)
         wc_bf = [held.tile([P, CB, HALF * P], BF16, name=f"wc_bf{half}") for half in range(2)]
-        nc.sync.dma_start(wc_bf[0][:, 0:HALF, :], wc_by_rows[:, 0:HALF, 0 : HALF * P])
+        for k in range(HALF):
+            nc.sync.dma_start(wc_bf[0][:, k, :], wc_by_rows[:, k, 0 : HALF * P])
         nc.sync.dma_start(wc_bf[0][:, HALF:CB, :], wc_by_rows[:, HALF:CB, 0 : HALF * P])
         offsets = held.tile([P, N // 16], U16, name="offsets")
         nc.sync.dma_start(offsets[:], offs)

@@ -26,8 +26,7 @@ def tile_attngcnlayer_kernel(tc, base, node, adj, wc, offs, out):
         nc.sync.dma_start(adj_bf[:], adj)
         wc_by_rows = wc.rearrange("(k p) c -> p k c", p=P)
         wc_bf = [held.tile([P, CB, HALF * P], BF16, name=f"wc_bf{half}") for half in range(2)]
-        for k in range(HALF):
-            nc.sync.dma_start(wc_bf[0][:, k, :], wc_by_rows[:, k, 0 : HALF * P])
+        nc.sync.dma_start(wc_bf[0][:, 0:HALF, :], wc_by_rows[:, 0:HALF, 0 : HALF * P])
         nc.sync.dma_start(wc_bf[0][:, HALF:CB, :], wc_by_rows[:, HALF:CB, 0 : HALF * P])
         offsets = held.tile([P, N // 16], U16, name="offsets")
         nc.sync.dma_start(offsets[:], offs)
@@ -45,8 +44,8 @@ def tile_attngcnlayer_kernel(tc, base, node, adj, wc, offs, out):
         nc.vector.reciprocal(inv_deg[:], deg_ps[:])
 
         node_bf = held.tile([P, CB, N], BF16, name="node_bf")
-        nc.vector.tensor_copy(node_bf[:, 0:HALF, :], node_f32[:, 0:HALF, :])
-        nc.vector.tensor_copy(node_bf[:, HALF:CB, :], node_f32[:, HALF:CB, :])
+        for k in range(CB):
+            nc.vector.tensor_copy(node_bf[:, k, :], node_f32[:, k, :])
 
         for b in range(CB):
             h_ps = psum.tile([P, P], F32, name="h_ps")

import concourse.mybir as mybir

F32, BF16, U16 = mybir.dt.float32, mybir.dt.bfloat16, mybir.dt.uint16
ADD, MULT = mybir.AluOpType.add, mybir.AluOpType.mult
COPY = mybir.ActivationFunctionType.Copy

P = 128
C, S, N = 512, 256, 128
CB = C // P
HALF = CB // 2

FLOPS = 2 * N * C * C + 2 * C * N * N


def tile_attngcnlayer_kernel(tc, base, node, adj, wc, offs, out):
    nc = tc.nc
    with (
        tc.tile_pool(name="held", bufs=1) as held,
        tc.psum_pool(name="psum_deg", bufs=1) as psum_deg,
        tc.psum_pool(name="psum", bufs=2) as psum,
    ):
        node_by_rows = node.rearrange("(k p) j -> p k j", p=P)
        node_f32 = held.tile([P, CB, N], F32, name="node_f32")
        nc.sync.dma_start(node_f32[:], node_by_rows)
        adj_bf = held.tile([P, N], BF16, name="adj_bf")
        nc.sync.dma_start(adj_bf[:], adj)
        wc_by_rows = wc.rearrange("(k p) c -> p k c", p=P)
        wc_bf = [held.tile([P, CB, HALF * P], BF16, name=f"wc_bf{half}") for half in range(2)]
        nc.sync.dma_start(wc_bf[0][:, 0:HALF, :], wc_by_rows[:, 0:HALF, 0 : HALF * P])
        nc.sync.dma_start(wc_bf[0][:, HALF:CB, :], wc_by_rows[:, HALF:CB, 0 : HALF * P])
        offsets = held.tile([P, N // 16], U16, name="offsets")
        nc.sync.dma_start(offsets[:], offs)
        windows = [held.tile([P, S], F32, name=f"window{b}") for b in range(CB)]
        nc.sync.dma_start(windows[0][:], base[0:P, :])
        nc.sync.dma_start(wc_bf[1][:], wc_by_rows[:, :, HALF * P : C])
        for b in range(1, CB):
            nc.sync.dma_start(windows[b][:], base[b * P : (b + 1) * P, :])

        ones = held.tile([P, P], BF16, name="ones")
        nc.gpsimd.memset(ones[:], 1.0)
        deg_ps = psum_deg.tile([P, N], F32, name="deg_ps")
        nc.tensor.matmul(deg_ps[:], ones[:], adj_bf[:], start=True, stop=True)
        inv_deg = held.tile([P, N], F32, name="inv_deg")
        nc.vector.reciprocal(inv_deg[:], deg_ps[:])

        node_bf = held.tile([P, CB, N], BF16, name="node_bf")
        for k in range(CB):
            nc.vector.tensor_copy(node_bf[:, k, :], node_f32[:, k, :])

        for b in range(CB):
            h_ps = psum.tile([P, P], F32, name="h_ps")
            wc_cols = wc_bf[b // HALF][:, :, (b % HALF) * P : (b % HALF + 1) * P]
            for k in range(CB):
                nc.tensor.matmul(h_ps[:], node_bf[:, k, :], wc_cols[:, k, :], start=(k == 0), stop=(k == CB - 1))
            h_bf = held.tile([P, P], BF16, name=f"h_bf{b}")
            nc.scalar.activation(h_bf[:], h_ps[:], COPY)

            ctx_ps = psum.tile([P, N], F32, name="ctx_ps")
            nc.tensor.matmul(ctx_ps[:], h_bf[:], adj_bf[:], start=True, stop=True)
            ctx = held.tile([P, N], F32, name=f"ctx{b}")
            nc.vector.tensor_tensor(ctx[:], ctx_ps[:], inv_deg[:], MULT)
            nc.vector.tensor_tensor(windows[b][:].indirect(offsets[:]), node_f32[:, b, :], ctx[:], ADD)
            nc.sync.dma_start(out[b * P : (b + 1) * P, :], windows[b][:])
